import numpy as np
import ml_dtypes


def mxq(x, axis, fmt="e4m3"):
    dtype, down = {"e4m3": (ml_dtypes.float8_e4m3fn, 7), "e5m2": (ml_dtypes.float8_e5m2, 14)}[fmt]
    v = np.moveaxis(np.asarray(x, np.float32).astype(ml_dtypes.bfloat16).astype(np.float64), axis, -1)
    blocks = v.reshape(v.shape[:-1] + (-1, 32))
    amax = np.abs(blocks).max(-1, keepdims=True)
    byte = np.maximum(np.where(amax > 0, np.frexp(amax)[1] - 1 + 127, 0) - down, 1)
    scale = np.exp2(byte - 127.0)
    codes = (blocks / scale).astype(np.float32).astype(dtype).astype(np.float64)
    return np.moveaxis((codes * scale).reshape(v.shape), -1, axis)


WIDE = False


def mx_kscale(k):
    if not WIDE:
        return np.ones(k)
    levels = np.array([30, -30])
    if k % 512:
        return np.exp2(np.random.permutation(np.resize(levels, k // 32))).repeat(32)
    a = np.empty((k // 512, 16))
    for p in range(k // 512):
        a[p, :8] = np.random.permutation(np.resize(levels, 8))
        for g in range(8):
            far = levels[np.abs(levels - a[p, g]) >= 10]
            a[p, g + 8] = far[np.random.randint(len(far))]
    return np.exp2(a.ravel()).repeat(32)


BF16 = ml_dtypes.bfloat16


def bf(x):
    return np.asarray(x, np.float32).astype(BF16)


def f64(x):
    return np.asarray(x).astype(np.float64)


E2M1 = np.array([0.0, 0.5, 1.0, 1.5, 2.0, 3.0, 4.0, 6.0, -0.0, -0.5, -1.0, -1.5, -2.0, -3.0, -4.0, -6.0])


def pack_weight(w, fmt):
    k, n = w.shape
    w = f64(bf(w)).reshape(k // 32, 32, n)
    amax = np.abs(w).max(1)
    if fmt == "e4m3":
        byte = np.frexp(amax)[1] - 1 + 127 - 7
    else:
        mant, ex = np.frexp(amax / 6.0)
        byte = np.where(mant > 0.5, ex, ex - 1) + 127
    byte = np.clip(np.where(amax > 0, byte, 1), 1, 254)
    scaled = (w * np.exp2(127.0 - byte)[:, None, :]).reshape(k, n).astype(np.float32)
    by_word = np.ascontiguousarray(scaled.reshape(k // 512, 128, 4, n).transpose(0, 1, 3, 2))
    if fmt == "e4m3":
        words = by_word.astype(ml_dtypes.float8_e4m3fn).view(np.uint8)
    else:
        c = by_word.astype(ml_dtypes.float4_e2m1fn).view(np.uint8) & 0xF
        words = c[..., 0::2] | (c[..., 1::2] << 4)
    return np.ascontiguousarray(words), np.ascontiguousarray(byte.astype(np.uint8).reshape(k // 512, 16, n))


def unpack_weight(words, scales, fmt):
    g, p, n, _ = words.shape
    if fmt == "e4m3":
        vals = np.ascontiguousarray(words).view(ml_dtypes.float8_e4m3fn).astype(np.float64)
    else:
        nib = np.empty((g, p, n, 4), np.uint8)
        nib[..., 0::2] = words & 0xF
        nib[..., 1::2] = words >> 4
        vals = E2M1[nib]
    vals = vals * np.repeat(np.exp2(scales.astype(np.float64) - 127.0), 8, axis=1)[..., None]
    return vals.transpose(0, 1, 3, 2).reshape(g * 512, n)

def pack4(w):
    words, scales = pack_weight(w, "e2m1")
    return words.reshape(words.shape[0], 128, -1), scales


def unpack4(words, scales):
    return unpack_weight(words.reshape(words.shape[0], 128, -1, 2), scales, "e2m1")


B, S, H, D = 2, 256, 12, 128
DIM = H * D
EPS = 1e-6
QK_RMS = 0.004


def rmsnorm(x, w):
    var = np.mean(x * x, axis=-1, keepdims=True)
    return x * (1.0 / np.sqrt(var + EPS)) * w


def apply_rope(x, freqs_cis):
    x_ = x.reshape(B, H, S, D // 2, 1, 2)
    out = freqs_cis[..., 0] * x_[..., 0] + freqs_cis[..., 1] * x_[..., 1]
    return out.reshape(B, H, S, D)


def heads(t):
    return t.reshape(B, S, H, D).transpose(0, 2, 1, 3)


def setup_inputs():
    s = mx_kscale(DIM)
    col = np.repeat(np.array([QK_RMS, QK_RMS, 1.0]), DIM)
    hidden_states = bf(np.random.standard_normal((B, S, DIM)) * s)
    image_rotary_emb = bf(np.random.standard_normal((1, 1, S, D // 2, 2, 2)))
    words, scales = pack4(np.random.standard_normal((DIM, 3 * DIM)) * col / np.sqrt(DIM) / s[:, None])
    return {"hidden_states": hidden_states,
            "image_rotary_emb": image_rotary_emb,
            "w_qkv_words": words,
            "w_qkv_scales": scales,
            "b_qkv": bf(np.random.standard_normal(3 * DIM) * 0.5 * col),
            "norm_q_w": bf(1.0 + 0.1 * np.random.standard_normal(D)),
            "norm_k_w": bf(1.0 + 0.1 * np.random.standard_normal(D))}


def reference(hidden_states, image_rotary_emb, w_qkv_words, w_qkv_scales, b_qkv, norm_q_w, norm_k_w):
    xq = mxq(f64(hidden_states), 2, "e5m2")
    w = unpack4(w_qkv_words, w_qkv_scales).reshape(DIM, 3, DIM)
    b = f64(b_qkv).reshape(3, DIM)
    f = f64(image_rotary_emb)
    q = heads((xq @ w[:, 0]) + b[0])
    k = heads((xq @ w[:, 1]) + b[1])
    v = heads((xq @ w[:, 2]) + b[2])
    q = apply_rope(rmsnorm(q, f64(norm_q_w)), f)
    k = apply_rope(rmsnorm(k, f64(norm_k_w)), f)
    return q, k, v

@@ -1,0 +1,284 @@
+from contextlib import ExitStack
+
+import concourse.mybir as mybir
+from concourse.masks import make_identity
+
+B, S, H, D = 2, 256, 12, 128
+DIM = H * D
+EPS = 1e-6
+FLOPS = 2 * B * S * DIM * 3 * DIM
+
+F32 = mybir.dt.float32
+BF16 = mybir.dt.bfloat16
+I32 = mybir.dt.int32
+U32 = mybir.dt.uint32
+U8 = mybir.dt.uint8
+E5M2X4 = mybir.dt.float8_e5m2_x4
+E2M1X4 = mybir.dt.float4_e2m1fn_x4
+ACT = mybir.ActivationFunctionType
+ALU = mybir.AluOpType
+
+P = 128
+PASSES = DIM // 512
+TOKENS = B * S
+BANK = 512
+NORMED_HEADS = 2 * H
+V0 = 2 * DIM
+CHUNKS = [(0, 768), (V0, V0 + 512), (768, DIM), (V0 + 512, 3 * DIM), (DIM, V0)]
+V_FIRST_STEP = 2
+
+
+def tile_fluxsingleattention_pa_kernel(
+    tc, hidden_states, image_rotary_emb, w_qkv_words, w_qkv_scales, b_qkv, norm_q_w, norm_k_w, out_0, out_1, out_2
+):
+    nc = tc.nc
+    with ExitStack() as ctx:
+        keep = ctx.enter_context(tc.tile_pool(name="keep", bufs=1))
+        work = ctx.enter_context(tc.tile_pool(name="work", bufs=4))
+        psum = ctx.enter_context(tc.psum_pool(name="psum", bufs=2))
+        ctx.enter_context(tc.manual_schedule())
+
+        rows = keep.tile([P, D], BF16, name="rows")
+        nc.vector.memset(rows[:].bitcast(I32), 0)
+        planes, words = [], []
+        for n, (c0, c1) in enumerate(CHUNKS):
+            plane = keep.tile([P, PASSES, c1 - c0], U8, name="plane%d" % n, align_bytes=64)
+            nc.vector.memset(plane[:].rearrange("p g n -> p (g n)").bitcast(I32), 0)
+            planes.append(plane)
+            word = keep.tile([P, PASSES, 2 * (c1 - c0)], U8, name="word%d" % n, align_bytes=64)
+            words.append(word)
+
+        nc.scalar.dma_start(out=rows[0 : 3 * H, :], in_=b_qkv.rearrange("(r d) -> r d", d=D))
+        nc.scalar.dma_start(out=rows[3 * H : 3 * H + 1, :], in_=norm_q_w.rearrange("(r d) -> r d", r=1))
+        nc.scalar.dma_start(out=rows[3 * H + 1 : 3 * H + 2, :], in_=norm_k_w.rearrange("(r d) -> r d", r=1))
+
+        x_sb = {}
+        for g in range(PASSES):
+            for b in range(B):
+                xt = keep.tile([P, 2, 512], BF16, name="x%d%d" % (g, b), align_bytes=64)
+                nc.sync.dma_start(
+                    out=xt[:], in_=hidden_states[b].rearrange("(p j) k -> p j k", j=2)[:, :, 512 * g : 512 * (g + 1)]
+                )
+                x_sb[(g, b)] = xt
+
+        def load_scales(n):
+            c0, c1 = CHUNKS[n]
+            for r in range(4):
+                nc.sync.dma_start(
+                    out=planes[n][r:P:32, :, :].bitcast(I32),
+                    in_=w_qkv_scales[:, r:16:4, c0:c1].rearrange("g q n -> q g n").bitcast(I32),
+                )
+
+        def load_words(n):
+            c0, c1 = CHUNKS[n]
+            nc.sync.dma_start(
+                out=words[n][:].bitcast(I32),
+                in_=w_qkv_words[:, :, 2 * c0 : 2 * c1].rearrange("g p n -> p g n").bitcast(I32),
+            )
+
+        load_scales(0)
+        load_words(0)
+        emb = keep.tile([P, 2, 2 * D], BF16, name="emb")
+        nc.sync.dma_start(out=emb[:], in_=image_rotary_emb[0, 0].rearrange("(s j) f i c -> s j (f i c)", j=2))
+        load_scales(1)
+        load_scales(2)
+        load_words(1)
+        load_words(2)
+        load_scales(3)
+        load_scales(4)
+        load_words(3)
+        load_words(4)
+
+        def weight(c0, width, g):
+            n = [m for m, (lo, hi) in enumerate(CHUNKS) if lo <= c0 < hi][0]
+            off = c0 - CHUNKS[n][0]
+            return (
+                words[n][:, g, 2 * off : 2 * (off + width)].bitcast(E2M1X4),
+                planes[n][:, g, off : off + width],
+            )
+
+        ident = keep.tile([P, P], F32, name="ident")
+        make_identity(nc, ident[:])
+        ident_bf = keep.tile([P, P], BF16, name="ident_bf")
+        nc.vector.tensor_copy(out=ident_bf[:], in_=ident[:])
+        split = keep.tile([P, 2, D // 2], F32, name="split")
+        nc.vector.tensor_copy(out=split[:], in_=ident[:].rearrange("p (f c) -> p c f", c=2))
+
+        codes, xscales = [], []
+        for g in range(PASSES):
+            code = keep.tile([P, TOKENS], U32, name="code%d" % g, align_bytes=64)
+            xscale = keep.tile([P, TOKENS], U8, name="xscale%d" % g, align_bytes=64)
+            codes.append(code)
+            xscales.append(xscale)
+        for g in range(PASSES):
+            for b in range(B):
+                bank = psum.tile([P, 2, 2, P], F32, name="xbank", tag="t", bufs=4)
+                xw = x_sb[(g, b)][:].bitcast(F32)
+                for j in range(2):
+                    for u in range(2):
+                        nc.tensor.transpose(bank[:, j, u, :], xw[:, j, u:256:2], ident[:])
+                grouped = work.tile([P, 2 * P * 4], BF16, name="grouped", align_bytes=64)
+                nc.scalar.copy(
+                    out=grouped[:].bitcast(F32).rearrange("p (j r u) -> p j r u", j=2, u=2),
+                    in_=bank[:].rearrange("p j u r -> p j r u"),
+                )
+                cols = slice(256 * b, 256 * (b + 1))
+                nc.vector.quantize_mx(out=codes[g][:, cols].bitcast(E5M2X4), scales=xscales[g][:, cols], in_=grouped[:])
+
+        small = psum.tile([P, 8, D], BF16, name="small", tag="v")
+        nc.tensor.transpose(small[:, 0, :], rows[:], ident_bf[:])
+        for m, row in enumerate([3 * H, 3 * H + 1] + list(range(2 * H, 2 * H + 4))):
+            nc.tensor.matmul(
+                small[:, 1 + m, :], lhsT=ident_bf[:, row : row + 1].to_broadcast([P, P]), rhs=rows[:], start=True, stop=True
+            )
+        spread = psum.tile([P, 8, D], BF16, name="spread", tag="v")
+        for m in range(8):
+            row = 2 * H + 4 + m
+            nc.tensor.matmul(
+                spread[:, m, :], lhsT=ident_bf[:, row : row + 1].to_broadcast([P, P]), rhs=rows[:], start=True, stop=True
+            )
+        bias_col = keep.tile([P, NORMED_HEADS], F32, name="bias_col")
+        nc.vector.tensor_copy(out=bias_col[:], in_=small[:, 0, 0:NORMED_HEADS])
+        table = keep.tile([P, 2, 2, 2 * D], F32, name="table")
+        for kind in range(2):
+            gain = small[:, 1 + kind, :].rearrange("s (f c) -> s c f", c=2).unsqueeze(3).broadcast_to([P, 2, D // 2, 2])
+            for j in range(2):
+                nc.vector.tensor_tensor(
+                    out=table[:, kind, j, :].rearrange("s (c f i) -> s c f i", c=2, i=2),
+                    in0=emb[:, j, :].rearrange("s (f i c) -> s c f i", i=2, c=2),
+                    in1=gain,
+                    op=ALU.mult,
+                )
+        bias_v = keep.tile([P, H, D], BF16, name="bias_v")
+        nc.vector.tensor_copy(out=bias_v[:, 0:4, :], in_=small[:, 3:7, :])
+        nc.vector.tensor_copy(out=bias_v[:, 4:H, :], in_=spread[:])
+
+        acc, y_t, turned, sumsq, root, rstd, prod, vacc, vout = {}, {}, {}, {}, {}, {}, {}, {}, {}
+
+        def project(h):
+            acc[h] = psum.tile([P, TOKENS], F32, name="acc", tag="f")
+            for g in range(PASSES):
+                w, ws = weight(D * h, D, g)
+                nc.tensor.matmul_mx(
+                    out=acc[h][:], lhsT=w, lhsT_scale=ws, rhs=codes[g][:].bitcast(E5M2X4), rhs_scale=xscales[g][:],
+                    start=(g == 0), stop=(g == PASSES - 1),
+                )
+
+        def add_bias(h):
+            y_t[h] = work.tile([P, TOKENS], F32, name="y_t")
+            nc.scalar.activation(out=y_t[h][:], in_=acc[h][:], func=ACT.Identity, bias=bias_col[:, h : h + 1], scale=1.0)
+
+        def turn(h):
+            turned[h] = psum.tile([P, 4, D], F32, name="turned", tag="t", bufs=4)
+            for t in range(4):
+                nc.tensor.transpose(
+                    turned[h][:, t, :], y_t[h][:, P * t : P * (t + 1)], split[:].rearrange("p c f -> p (c f)")
+                )
+
+        def squares(h, tiles):
+            if h not in sumsq:
+                sumsq[h] = work.tile([P, 4], F32, name="sumsq")
+            for t in tiles:
+                squared = work.tile([P, D], F32, name="squared")
+                nc.scalar.activation(
+                    out=squared[:], in_=turned[h][:, t, :], func=ACT.Square, accum_out=sumsq[h][:, t : t + 1]
+                )
+
+        def take_root(h):
+            root[h] = work.tile([P, 4], F32, name="root")
+            nc.scalar.activation(out=root[h][:], in_=sumsq[h][:], func=ACT.Sqrt, scale=1.0 / D, bias=EPS)
+
+        def invert(h):
+            rstd[h] = work.tile([P, 4], F32, name="rstd")
+            nc.vector.reciprocal(out=rstd[h][:], in_=root[h][:])
+
+        def rope_products(h, tiles):
+            if h not in prod:
+                prod[h] = work.tile([P, 4, 2, D], F32, name="prod")
+            for t in tiles:
+                nc.vector.scalar_tensor_tensor(
+                    out=prod[h][:, t, :, :].rearrange("s c (f i) -> s (c f) i", i=2),
+                    in0=turned[h][:, t, :].unsqueeze(2).broadcast_to([P, D, 2]),
+                    scalar=rstd[h][:, t : t + 1],
+                    in1=table[:, h // H, t % 2, :].rearrange("s (m i) -> s m i", i=2),
+                    op0=ALU.mult,
+                    op1=ALU.mult,
+                )
+
+        def rope_sum(h):
+            res = keep.tile([P, 4, D], F32, name="res%d" % h)
+            nc.gpsimd.tensor_tensor(out=res[:], in0=prod[h][:, :, 0, :], in1=prod[h][:, :, 1, :], op=ALU.add)
+            dst = (out_0, out_1)[h // H]
+            nc.sync.dma_start(
+                out=dst[:, h % H].rearrange("b (p j) d -> p b (j d)", j=2),
+                in_=res[:].rearrange("p (b j) d -> p b (j d)", j=2),
+            )
+
+        def project_v(n):
+            c, t = divmod(n, 4)
+            vacc[n] = psum.tile([P, BANK], F32, name="vacc", tag="v")
+            cols = slice(P * t, P * (t + 1))
+            for g in range(PASSES):
+                w, ws = weight(V0 + BANK * c, BANK, g)
+                nc.tensor.matmul_mx(
+                    out=vacc[n][:], lhsT=codes[g][:, cols].bitcast(E5M2X4), lhsT_scale=xscales[g][:, cols],
+                    rhs=w, rhs_scale=ws, start=(g == 0), stop=(g == PASSES - 1),
+                )
+
+        def finish_v(n):
+            c, t = divmod(n, 4)
+            b, j = divmod(t, 2)
+            if j == 0:
+                vout[n // 2] = keep.tile([P, 4, 2, D], F32, name="vout%d" % (n // 2))
+            nc.vector.tensor_tensor(
+                out=vout[n // 2][:, :, j, :],
+                in0=vacc[n][:].rearrange("p (h d) -> p h d", d=D),
+                in1=bias_v[:, 4 * c : 4 * (c + 1), :],
+                op=ALU.add,
+            )
+            if j == 1:
+                nc.sync.dma_start(
+                    out=out_2[b, 4 * c : 4 * (c + 1)].rearrange("h (p j) d -> p h (j d)", j=2),
+                    in_=vout[n // 2][:].rearrange("p h j d -> p h (j d)"),
+                )
+
+        steps = NORMED_HEADS // 2
+        project(0)
+        add_bias(0)
+        for i in range(steps + 1):
+            a, b2 = 2 * i - 2, 2 * i - 1
+            v_now = i - V_FIRST_STEP
+            if i < steps:
+                project(2 * i + 1)
+            if 2 * i + 2 < NORMED_HEADS:
+                project(2 * i + 2)
+            if v_now >= 0:
+                project_v(v_now)
+            if i == steps:
+                project_v(v_now + 1)
+            if i > 0:
+                squares(a, range(4))
+                squares(b2, range(1))
+                take_root(a)
+                squares(b2, range(1, 4))
+            if i < steps:
+                add_bias(2 * i + 1)
+            if i > 0:
+                take_root(b2)
+            if 2 * i + 2 < NORMED_HEADS:
+                add_bias(2 * i + 2)
+            if i < steps:
+                turn(2 * i)
+                turn(2 * i + 1)
+            if i > 0:
+                invert(a)
+                rope_products(a, range(3))
+                invert(b2)
+                rope_products(a, range(3, 4))
+                rope_sum(a)
+                rope_products(b2, range(4))
+                rope_sum(b2)
+            if v_now >= 0:
+                finish_v(v_now)
+            if i == steps:
+                finish_v(v_now + 1)

@@ -24,8 +24,14 @@ TOKENS = B * S
 BANK = 512
 NORMED_HEADS = 2 * H
 V0 = 2 * DIM
-CHUNKS = [(0, 768), (V0, V0 + 512), (768, DIM), (V0 + 512, 3 * DIM), (DIM, V0)]
-V_FIRST_STEP = 2
+X_FIRST = 2
+PRO = 3
+AHEAD = 1
+CHUNKS = [(0, PRO * D), (PRO * D, DIM), (V0, 3 * DIM), (DIM, V0)]
+EARLY_TURN = False
+TAIL_V_FIRST = False
+RUNS = [2] * 11 + [1, 1]
+V_PER_RUN = [0, 0, 0, 1, 1, 1, 1, 1, 1, 1, 1, 1, 1, 2]
 
 
 def tile_fluxsingleattention_pa_kernel(
@@ -48,18 +54,19 @@ def tile_fluxsingleattention_pa_kernel(
             word = keep.tile([P, PASSES, 2 * (c1 - c0)], U8, name="word%d" % n, align_bytes=64)
             words.append(word)
 
-        nc.scalar.dma_start(out=rows[0 : 3 * H, :], in_=b_qkv.rearrange("(r d) -> r d", d=D))
-        nc.scalar.dma_start(out=rows[3 * H : 3 * H + 1, :], in_=norm_q_w.rearrange("(r d) -> r d", r=1))
-        nc.scalar.dma_start(out=rows[3 * H + 1 : 3 * H + 2, :], in_=norm_k_w.rearrange("(r d) -> r d", r=1))
-
         x_sb = {}
-        for g in range(PASSES):
+
+        def load_x(g):
             for b in range(B):
                 xt = keep.tile([P, 2, 512], BF16, name="x%d%d" % (g, b), align_bytes=64)
                 nc.sync.dma_start(
                     out=xt[:], in_=hidden_states[b].rearrange("(p j) k -> p j k", j=2)[:, :, 512 * g : 512 * (g + 1)]
                 )
                 x_sb[(g, b)] = xt
+
+        for g in range(X_FIRST):
+            load_x(g)
+        nc.scalar.dma_start(out=rows[0:NORMED_HEADS, :], in_=b_qkv[0:V0].rearrange("(r d) -> r d", d=D))
 
         def load_scales(n):
             c0, c1 = CHUNKS[n]
@@ -78,16 +85,23 @@ def tile_fluxsingleattention_pa_kernel(
 
         load_scales(0)
         load_words(0)
+        for g in range(X_FIRST, PASSES):
+            load_x(g)
         emb = keep.tile([P, 2, 2 * D], BF16, name="emb")
         nc.sync.dma_start(out=emb[:], in_=image_rotary_emb[0, 0].rearrange("(s j) f i c -> s j (f i c)", j=2))
+        gains = []
+        for kind, vec in enumerate((norm_q_w, norm_k_w)):
+            gain = keep.tile([P, D], BF16, name="gain%d" % kind)
+            nc.sync.dma_start(out=gain[:], in_=vec.partition_broadcast(P))
+            gains.append(gain)
         load_scales(1)
-        load_scales(2)
         load_words(1)
+        load_scales(2)
         load_words(2)
+        bias_v = keep.tile([P, DIM], BF16, name="bias_v")
+        nc.sync.dma_start(out=bias_v[:], in_=b_qkv[V0 : 3 * DIM].partition_broadcast(P))
         load_scales(3)
-        load_scales(4)
         load_words(3)
-        load_words(4)
 
         def weight(c0, width, g):
             n = [m for m, (lo, hi) in enumerate(CHUNKS) if lo <= c0 < hi][0]
@@ -110,7 +124,7 @@ def tile_fluxsingleattention_pa_kernel(
             xscale = keep.tile([P, TOKENS], U8, name="xscale%d" % g, align_bytes=64)
             codes.append(code)
             xscales.append(xscale)
-        for g in range(PASSES):
+        def prepare_x(g):
             for b in range(B):
                 bank = psum.tile([P, 2, 2, P], F32, name="xbank", tag="t", bufs=4)
                 xw = x_sb[(g, b)][:].bitcast(F32)
@@ -125,23 +139,18 @@ def tile_fluxsingleattention_pa_kernel(
                 cols = slice(256 * b, 256 * (b + 1))
                 nc.vector.quantize_mx(out=codes[g][:, cols].bitcast(E5M2X4), scales=xscales[g][:, cols], in_=grouped[:])
 
-        small = psum.tile([P, 8, D], BF16, name="small", tag="v")
-        nc.tensor.transpose(small[:, 0, :], rows[:], ident_bf[:])
-        for m, row in enumerate([3 * H, 3 * H + 1] + list(range(2 * H, 2 * H + 4))):
-            nc.tensor.matmul(
-                small[:, 1 + m, :], lhsT=ident_bf[:, row : row + 1].to_broadcast([P, P]), rhs=rows[:], start=True, stop=True
-            )
-        spread = psum.tile([P, 8, D], BF16, name="spread", tag="v")
-        for m in range(8):
-            row = 2 * H + 4 + m
-            nc.tensor.matmul(
-                spread[:, m, :], lhsT=ident_bf[:, row : row + 1].to_broadcast([P, P]), rhs=rows[:], start=True, stop=True
-            )
         bias_col = keep.tile([P, NORMED_HEADS], F32, name="bias_col")
-        nc.vector.tensor_copy(out=bias_col[:], in_=small[:, 0, 0:NORMED_HEADS])
+
+        def prepare_bias():
+            if True:
+                bias_t = psum.tile([P, D], BF16, name="bias_t", tag="v")
+                nc.tensor.transpose(bias_t[:], rows[:], ident_bf[:])
+                nc.vector.tensor_copy(out=bias_col[:], in_=bias_t[:, 0:NORMED_HEADS])
+
         table = keep.tile([P, 2, 2, 2 * D], F32, name="table")
-        for kind in range(2):
-            gain = small[:, 1 + kind, :].rearrange("s (f c) -> s c f", c=2).unsqueeze(3).broadcast_to([P, 2, D // 2, 2])
+
+        def prepare_table(kind):
+            gain = gains[kind][:].rearrange("s (f c) -> s c f", c=2).unsqueeze(3).broadcast_to([P, 2, D // 2, 2])
             for j in range(2):
                 nc.vector.tensor_tensor(
                     out=table[:, kind, j, :].rearrange("s (c f i) -> s c f i", c=2, i=2),
@@ -149,15 +158,13 @@ def tile_fluxsingleattention_pa_kernel(
                     in1=gain,
                     op=ALU.mult,
                 )
-        bias_v = keep.tile([P, H, D], BF16, name="bias_v")
-        nc.vector.tensor_copy(out=bias_v[:, 0:4, :], in_=small[:, 3:7, :])
-        nc.vector.tensor_copy(out=bias_v[:, 4:H, :], in_=spread[:])
 
-        acc, y_t, turned, sumsq, root, rstd, prod, vacc, vout = {}, {}, {}, {}, {}, {}, {}, {}, {}
+        acc, y_t, turned, sumsq, rstd, prod, vacc, res = {}, {}, {}, {}, {}, {}, {}, {}
 
-        def project(h):
-            acc[h] = psum.tile([P, TOKENS], F32, name="acc", tag="f")
-            for g in range(PASSES):
+        def project(h, passes=range(PASSES)):
+            if h not in acc:
+                acc[h] = psum.tile([P, TOKENS], F32, name="acc", tag="v" if 2 <= h < PRO else "f")
+            for g in passes:
                 w, ws = weight(D * h, D, g)
                 nc.tensor.matmul_mx(
                     out=acc[h][:], lhsT=w, lhsT_scale=ws, rhs=codes[g][:].bitcast(E5M2X4), rhs_scale=xscales[g][:],
@@ -168,117 +175,166 @@ def tile_fluxsingleattention_pa_kernel(
             y_t[h] = work.tile([P, TOKENS], F32, name="y_t")
             nc.scalar.activation(out=y_t[h][:], in_=acc[h][:], func=ACT.Identity, bias=bias_col[:, h : h + 1], scale=1.0)
 
-        def turn(h):
-            turned[h] = psum.tile([P, 4, D], F32, name="turned", tag="t", bufs=4)
-            for t in range(4):
+        def tiles_of(unit):
+            h, batches = unit
+            return [2 * b + j for b in batches for j in range(2)]
+
+        def turn(unit):
+            tiles = tiles_of(unit)
+            turned[unit] = psum.tile([P, len(tiles), D], F32, name="turned", tag="t", bufs=4)
+            for n, t in enumerate(tiles):
                 nc.tensor.transpose(
-                    turned[h][:, t, :], y_t[h][:, P * t : P * (t + 1)], split[:].rearrange("p c f -> p (c f)")
+                    turned[unit][:, n, :], y_t[unit[0]][:, P * t : P * (t + 1)], split[:].rearrange("p c f -> p (c f)")
                 )
 
-        def squares(h, tiles):
-            if h not in sumsq:
-                sumsq[h] = work.tile([P, 4], F32, name="sumsq")
-            for t in tiles:
+        def squares(unit, lo, hi=4):
+            count = len(tiles_of(unit))
+            if unit not in sumsq:
+                sumsq[unit] = work.tile([P, count], F32, name="sumsq")
+            for n in range(lo, min(hi, count)):
                 squared = work.tile([P, D], F32, name="squared")
                 nc.scalar.activation(
-                    out=squared[:], in_=turned[h][:, t, :], func=ACT.Square, accum_out=sumsq[h][:, t : t + 1]
+                    out=squared[:], in_=turned[unit][:, n, :], func=ACT.Square, accum_out=sumsq[unit][:, n : n + 1]
                 )
 
-        def take_root(h):
-            root[h] = work.tile([P, 4], F32, name="root")
-            nc.scalar.activation(out=root[h][:], in_=sumsq[h][:], func=ACT.Sqrt, scale=1.0 / D, bias=EPS)
+        def inverse_root(unit):
+            rstd[unit] = work.tile([P, len(tiles_of(unit))], F32, name="rstd")
+            nc.scalar.activation(
+                out=rstd[unit][:], in_=sumsq[unit][:], func=ACT.Abs_reciprocal_sqrt, scale=1.0 / D, bias=EPS
+            )
 
-        def invert(h):
-            rstd[h] = work.tile([P, 4], F32, name="rstd")
-            nc.vector.reciprocal(out=rstd[h][:], in_=root[h][:])
-
-        def rope_products(h, tiles):
-            if h not in prod:
-                prod[h] = work.tile([P, 4, 2, D], F32, name="prod")
-            for t in tiles:
+        def rope_products(unit):
+            tiles = tiles_of(unit)
+            prod[unit] = work.tile([P, len(tiles), 2, D], F32, name="prod")
+            for n, t in enumerate(tiles):
                 nc.vector.scalar_tensor_tensor(
-                    out=prod[h][:, t, :, :].rearrange("s c (f i) -> s (c f) i", i=2),
-                    in0=turned[h][:, t, :].unsqueeze(2).broadcast_to([P, D, 2]),
-                    scalar=rstd[h][:, t : t + 1],
-                    in1=table[:, h // H, t % 2, :].rearrange("s (m i) -> s m i", i=2),
+                    out=prod[unit][:, n, :, :].rearrange("s c (f i) -> s (c f) i", i=2),
+                    in0=turned[unit][:, n, :].unsqueeze(2).broadcast_to([P, D, 2]),
+                    scalar=rstd[unit][:, n : n + 1],
+                    in1=table[:, unit[0] // H, t % 2, :].rearrange("s (m i) -> s m i", i=2),
                     op0=ALU.mult,
                     op1=ALU.mult,
                 )
 
-        def rope_sum(h):
-            res = keep.tile([P, 4, D], F32, name="res%d" % h)
-            nc.gpsimd.tensor_tensor(out=res[:], in0=prod[h][:, :, 0, :], in1=prod[h][:, :, 1, :], op=ALU.add)
+        def rope_sum(unit, engine):
+            h, batches = unit
+            res[unit] = keep.tile([P, 2 * len(batches), D], F32, name="res%d_%d" % (h, batches[0]))
+            engine.tensor_tensor(out=res[unit][:], in0=prod[unit][:, :, 0, :], in1=prod[unit][:, :, 1, :], op=ALU.add)
+
+        def store_head(unit):
+            h, batches = unit
             dst = (out_0, out_1)[h // H]
             nc.sync.dma_start(
-                out=dst[:, h % H].rearrange("b (p j) d -> p b (j d)", j=2),
-                in_=res[:].rearrange("p (b j) d -> p b (j d)", j=2),
+                out=dst[batches[0] : batches[-1] + 1, h % H].rearrange("b (p j) d -> p b (j d)", j=2),
+                in_=res[unit][:].rearrange("p (b j) d -> p b (j d)", j=2),
             )
 
-        def project_v(n):
-            c, t = divmod(n, 4)
-            vacc[n] = psum.tile([P, BANK], F32, name="vacc", tag="v")
-            cols = slice(P * t, P * (t + 1))
-            for g in range(PASSES):
-                w, ws = weight(V0 + BANK * c, BANK, g)
-                nc.tensor.matmul_mx(
-                    out=vacc[n][:], lhsT=codes[g][:, cols].bitcast(E5M2X4), lhsT_scale=xscales[g][:, cols],
-                    rhs=w, rhs_scale=ws, start=(g == 0), stop=(g == PASSES - 1),
-                )
+        def project_v(n, tag):
+            pair, b = divmod(n, B)
+            vacc[n] = psum.tile([P, 2, 2 * D], F32, name="vacc", tag=tag)
+            for j in range(2):
+                cols = slice(P * (2 * b + j), P * (2 * b + j + 1))
+                for g in range(PASSES):
+                    w, ws = weight(V0 + 2 * D * pair, 2 * D, g)
+                    nc.tensor.matmul_mx(
+                        out=vacc[n][:, j, :], lhsT=codes[g][:, cols].bitcast(E5M2X4), lhsT_scale=xscales[g][:, cols],
+                        rhs=w, rhs_scale=ws, start=(g == 0), stop=(g == PASSES - 1),
+                    )
 
         def finish_v(n):
-            c, t = divmod(n, 4)
-            b, j = divmod(t, 2)
-            if j == 0:
-                vout[n // 2] = keep.tile([P, 4, 2, D], F32, name="vout%d" % (n // 2))
+            pair, b = divmod(n, B)
+            vout = keep.tile([P, 2, 2, D], F32, name="vout%d" % n)
+            bias = bias_v[:, 2 * D * pair : 2 * D * (pair + 1)].rearrange("p (h d) -> p h d", d=D)
             nc.vector.tensor_tensor(
-                out=vout[n // 2][:, :, j, :],
-                in0=vacc[n][:].rearrange("p (h d) -> p h d", d=D),
-                in1=bias_v[:, 4 * c : 4 * (c + 1), :],
+                out=vout[:],
+                in0=vacc[n][:].rearrange("p j (h d) -> p h j d", d=D),
+                in1=bias.unsqueeze(2).broadcast_to([P, 2, 2, D]),
                 op=ALU.add,
             )
-            if j == 1:
-                nc.sync.dma_start(
-                    out=out_2[b, 4 * c : 4 * (c + 1)].rearrange("h (p j) d -> p h (j d)", j=2),
-                    in_=vout[n // 2][:].rearrange("p h j d -> p h (j d)"),
-                )
+            nc.sync.dma_start(
+                out=out_2[b, 2 * pair : 2 * (pair + 1)].rearrange("h (p j) d -> p h (j d)", j=2),
+                in_=vout[:].rearrange("p h j d -> p h (j d)"),
+            )
 
-        steps = NORMED_HEADS // 2
-        project(0)
-        add_bias(0)
-        for i in range(steps + 1):
-            a, b2 = 2 * i - 2, 2 * i - 1
-            v_now = i - V_FIRST_STEP
-            if i < steps:
-                project(2 * i + 1)
-            if 2 * i + 2 < NORMED_HEADS:
-                project(2 * i + 2)
-            if v_now >= 0:
-                project_v(v_now)
-            if i == steps:
-                project_v(v_now + 1)
-            if i > 0:
-                squares(a, range(4))
-                squares(b2, range(1))
-                take_root(a)
-                squares(b2, range(1, 4))
-            if i < steps:
-                add_bias(2 * i + 1)
-            if i > 0:
-                take_root(b2)
-            if 2 * i + 2 < NORMED_HEADS:
-                add_bias(2 * i + 2)
-            if i < steps:
-                turn(2 * i)
-                turn(2 * i + 1)
-            if i > 0:
-                invert(a)
-                rope_products(a, range(3))
-                invert(b2)
-                rope_products(a, range(3, 4))
-                rope_sum(a)
-                rope_products(b2, range(4))
-                rope_sum(b2)
-            if v_now >= 0:
-                finish_v(v_now)
-            if i == steps:
-                finish_v(v_now + 1)
+        prepare_x(0)
+        prepare_x(1)
+        prepare_bias()
+        early = 2 if X_FIRST < PASSES else 0
+        for h in range(early):
+            project(h, [0])
+        prepare_x(2)
+        prepare_table(0)
+        prepare_table(1)
+        for h in range(early, PRO):
+            project(h, [0])
+        for g in range(1, PASSES):
+            for h in range(PRO):
+                project(h, [g])
+        for h in range(AHEAD):
+            add_bias(h)
+        first = 0
+        old = []
+        next_v = 0
+        for r, n_v in enumerate(V_PER_RUN):
+            last = r == len(RUNS)
+            run = [] if last else list(range(first, first + RUNS[r]))
+            first += len(run)
+            new = [h + AHEAD for h in run if h + AHEAD < NORMED_HEADS]
+            run = [(h, (0, 1)) for h in run]
+            if r == len(RUNS) - 1:
+                run = run[:-1] + [(NORMED_HEADS - 1, (b,)) for b in range(B)]
+            vs = list(range(next_v, next_v + n_v))
+            next_v += n_v
+            todo_v = list(vs)
+            pending_store = []
+            done_v = 0
+            for m in range(max(len(old), len(new), 1)):
+                if m == 0:
+                    for h in new[:2]:
+                        if h not in acc:
+                            project(h)
+                    if len(new) < 2 and todo_v and not EARLY_TURN:
+                        n = todo_v.pop(0)
+                        project_v(n, "v")
+                elif m + 1 < len(new):
+                    if todo_v:
+                        n = todo_v.pop(0)
+                        project_v(n, "v")
+                    if new[m + 1] not in acc:
+                        project(new[m + 1])
+                if m == 0 and old:
+                    squares(old[0], 0)
+                    if len(old) > 1:
+                        squares(old[1], 0, 1)
+                    inverse_root(old[0])
+                    if len(old) > 1:
+                        squares(old[1], 1)
+                elif 0 < m and m + 1 < len(old):
+                    squares(old[m + 1], 0)
+                if m < len(new):
+                    add_bias(new[m])
+                if m + 1 < len(old):
+                    inverse_root(old[m + 1])
+                if m < len(old):
+                    if last and m == 0 and TAIL_V_FIRST:
+                        for n in vs:
+                            project_v(n, "f")
+                            finish_v(n)
+                        vs, todo_v = [], []
+                    rope_products(old[m])
+                    rope_sum(old[m], nc.vector if last and m == len(old) - 1 else nc.gpsimd)
+                    if m + 1 < len(old) or not vs or last:
+                        store_head(old[m])
+                    else:
+                        pending_store.append(old[m])
+            for k, n in enumerate(todo_v):
+                project_v(n, "f" if (last and k % 2 == 0) else "v")
+            for h in run:
+                turn(h)
+            for n in vs[:1]:
+                finish_v(n)
+            for h in pending_store:
+                store_head(h)
+            for n in vs[1:]:
+                finish_v(n)
+            old = run

@@ -19,19 +19,18 @@ ACT = mybir.ActivationFunctionType
 ALU = mybir.AluOpType
 
 P = 128
-PASSES = DIM // 512
+K_PASS = 512
+PASSES = DIM // K_PASS
 TOKENS = B * S
-BANK = 512
-NORMED_HEADS = 2 * H
-V0 = 2 * DIM
-X_FIRST = 2
-PRO = 3
-AHEAD = 1
-CHUNKS = [(0, PRO * D), (PRO * D, DIM), (V0, 3 * DIM), (DIM, V0)]
-EARLY_TURN = False
-TAIL_V_FIRST = False
-RUNS = [2] * 11 + [1, 1]
-V_PER_RUN = [0, 0, 0, 1, 1, 1, 1, 1, 1, 1, 1, 1, 1, 2]
+TILES = TOKENS // P
+K0, V0, HEADS = H, 2 * H, 3 * H
+
+EARLY = 4
+CHUNKS = [(K0, K0 + EARLY), (V0, V0 + EARLY), (K0 + EARLY, V0), (0, K0), (V0 + EARLY, HEADS)]
+QUADRANT = 32
+LATE_ROWS = HEADS - QUADRANT
+BANKS = {"turn": 4, "unit": 2, "v": 2}
+STAGE_BUFS = 4
 
 
 def tile_fluxsingleattention_pa_kernel(
@@ -40,301 +39,343 @@ def tile_fluxsingleattention_pa_kernel(
     nc = tc.nc
     with ExitStack() as ctx:
         keep = ctx.enter_context(tc.tile_pool(name="keep", bufs=1))
-        work = ctx.enter_context(tc.tile_pool(name="work", bufs=4))
-        psum = ctx.enter_context(tc.psum_pool(name="psum", bufs=2))
+        stage = ctx.enter_context(tc.tile_pool(name="stage", bufs=STAGE_BUFS))
+        psum = ctx.enter_context(tc.psum_pool(name="psum", bufs=1))
         ctx.enter_context(tc.manual_schedule())
 
-        rows = keep.tile([P, D], BF16, name="rows")
-        nc.vector.memset(rows[:].bitcast(I32), 0)
+        def bank(shape, dtype, role):
+            return psum.tile(shape, dtype, name="bank_" + role, tag=role, bufs=BANKS[role])
+
+        bias_by_head = b_qkv.rearrange("(h d) -> h d", d=D)
+        first_rows = keep.tile([P, D], BF16, name="first_rows")
+        late_rows = keep.tile([P, D], BF16, name="late_rows")
+        nc.sync.dma_start(out=first_rows[0:QUADRANT, :], in_=bias_by_head[LATE_ROWS:HEADS, :])
+        nc.vector.memset(first_rows[QUADRANT : 2 * QUADRANT, :].bitcast(I32), 0)
+        nc.vector.memset(first_rows[2 * QUADRANT : P, :].bitcast(I32), 0)
+        nc.vector.memset(late_rows[:].bitcast(I32), 0)
+
         planes, words = [], []
-        for n, (c0, c1) in enumerate(CHUNKS):
-            plane = keep.tile([P, PASSES, c1 - c0], U8, name="plane%d" % n, align_bytes=64)
-            nc.vector.memset(plane[:].rearrange("p g n -> p (g n)").bitcast(I32), 0)
-            planes.append(plane)
-            word = keep.tile([P, PASSES, 2 * (c1 - c0)], U8, name="word%d" % n, align_bytes=64)
-            words.append(word)
+        for n, (h0, h1) in enumerate(CHUNKS):
+            planes.append(keep.tile([P, PASSES, D * (h1 - h0)], U8, name="plane%d" % n, align_bytes=64))
+            words.append(keep.tile([P, PASSES, 2 * D * (h1 - h0)], U8, name="words%d" % n, align_bytes=64))
 
-        x_sb = {}
+        def clear_plane(n):
+            nc.vector.memset(planes[n][:].rearrange("p g n -> p (g n)").bitcast(I32), 0)
 
-        def load_x(g):
-            for b in range(B):
-                xt = keep.tile([P, 2, 512], BF16, name="x%d%d" % (g, b), align_bytes=64)
-                nc.sync.dma_start(
-                    out=xt[:], in_=hidden_states[b].rearrange("(p j) k -> p j k", j=2)[:, :, 512 * g : 512 * (g + 1)]
-                )
-                x_sb[(g, b)] = xt
+        clear_plane(0)
+        ident = keep.tile([P, P], F32, name="ident")
+        make_identity(nc, ident[:])
+        clear_plane(1)
+        ident_bf = keep.tile([P, P], BF16, name="ident_bf")
+        nc.vector.tensor_copy(out=ident_bf[:], in_=ident[:])
+        for n in range(2, len(CHUNKS)):
+            clear_plane(n)
 
-        for g in range(X_FIRST):
-            load_x(g)
-        nc.scalar.dma_start(out=rows[0:NORMED_HEADS, :], in_=b_qkv[0:V0].rearrange("(r d) -> r d", d=D))
+        x_pairs = {}
+
+        def load_x(b, g0, g1):
+            x_sb = keep.tile([P, 2, K_PASS * (g1 - g0)], BF16, name="x%d%d" % (b, g0), align_bytes=64)
+            tokens = hidden_states[b].rearrange("(p j) k -> p j k", j=2)
+            nc.sync.dma_start(out=x_sb[:], in_=tokens[:, :, K_PASS * g0 : K_PASS * g1])
+            width = K_PASS // 2
+            for g in range(g0, g1):
+                x_pairs[(b, g)] = x_sb[:].bitcast(F32)[:, :, width * (g - g0) : width * (g - g0 + 1)]
 
         def load_scales(n):
-            c0, c1 = CHUNKS[n]
+            h0, h1 = CHUNKS[n]
             for r in range(4):
                 nc.sync.dma_start(
-                    out=planes[n][r:P:32, :, :].bitcast(I32),
-                    in_=w_qkv_scales[:, r:16:4, c0:c1].rearrange("g q n -> q g n").bitcast(I32),
+                    out=planes[n][r:P:QUADRANT, :, :].bitcast(I32),
+                    in_=w_qkv_scales[:, r:16:4, D * h0 : D * h1].rearrange("g q n -> q g n").bitcast(I32),
                 )
 
         def load_words(n):
-            c0, c1 = CHUNKS[n]
+            h0, h1 = CHUNKS[n]
             nc.sync.dma_start(
                 out=words[n][:].bitcast(I32),
-                in_=w_qkv_words[:, :, 2 * c0 : 2 * c1].rearrange("g p n -> p g n").bitcast(I32),
+                in_=w_qkv_words[:, :, 2 * D * h0 : 2 * D * h1].rearrange("g p n -> p g n").bitcast(I32),
             )
 
+        load_x(0, 0, 1)
+        load_x(0, 1, PASSES)
         load_scales(0)
         load_words(0)
-        for g in range(X_FIRST, PASSES):
-            load_x(g)
+        nc.sync.dma_start(out=late_rows[0:LATE_ROWS, :], in_=bias_by_head[0:LATE_ROWS, :])
+        for kind, gain in enumerate((norm_q_w, norm_k_w)):
+            row = LATE_ROWS + kind
+            nc.sync.dma_start(out=late_rows[row : row + 1, :], in_=gain.rearrange("(r d) -> r d", r=1))
         emb = keep.tile([P, 2, 2 * D], BF16, name="emb")
-        nc.sync.dma_start(out=emb[:], in_=image_rotary_emb[0, 0].rearrange("(s j) f i c -> s j (f i c)", j=2))
-        gains = []
-        for kind, vec in enumerate((norm_q_w, norm_k_w)):
-            gain = keep.tile([P, D], BF16, name="gain%d" % kind)
-            nc.sync.dma_start(out=gain[:], in_=vec.partition_broadcast(P))
-            gains.append(gain)
-        load_scales(1)
-        load_words(1)
-        load_scales(2)
-        load_words(2)
-        bias_v = keep.tile([P, DIM], BF16, name="bias_v")
-        nc.sync.dma_start(out=bias_v[:], in_=b_qkv[V0 : 3 * DIM].partition_broadcast(P))
-        load_scales(3)
-        load_words(3)
+        nc.sync.dma_start(out=emb[:], in_=image_rotary_emb[0, 0].rearrange("(p j) f i c -> p j (f i c)", j=2))
+        load_x(1, 0, PASSES)
+        for n in (1, 2):
+            load_scales(n)
+            load_words(n)
+        for n in (3, 4):
+            load_scales(n)
+        for n in (3, 4):
+            load_words(n)
 
-        def weight(c0, width, g):
-            n = [m for m, (lo, hi) in enumerate(CHUNKS) if lo <= c0 < hi][0]
-            off = c0 - CHUNKS[n][0]
-            return (
-                words[n][:, g, 2 * off : 2 * (off + width)].bitcast(E2M1X4),
-                planes[n][:, g, off : off + width],
+        even_odd = keep.tile([P, 2, D // 2], F32, name="even_odd")
+        nc.scalar.activation(out=even_odd[:], in_=ident[:].rearrange("p (f c) -> p c f", c=2), func=ACT.Copy)
+
+        def weight(head, count, g):
+            n = [m for m, (h0, h1) in enumerate(CHUNKS) if h0 <= head < h1][0]
+            c0 = D * (head - CHUNKS[n][0])
+            c1 = c0 + D * count
+            return words[n][:, g, 2 * c0 : 2 * c1].bitcast(E2M1X4), planes[n][:, g, c0:c1]
+
+        codes, x_scales = [], []
+        for g in range(PASSES):
+            codes.append(keep.tile([P, TOKENS], U32, name="codes%d" % g, align_bytes=64))
+            x_scales.append(keep.tile([P, TOKENS], U8, name="x_scales%d" % g, align_bytes=64))
+        x_turned, x_grouped = {}, {}
+
+        def turn_x(b, g):
+            x_turned[(b, g)] = bank([P, 2, 2, P], F32, "turn")
+            for j in range(2):
+                for u in range(2):
+                    nc.tensor.transpose(x_turned[(b, g)][:, j, u, :], x_pairs[(b, g)][:, j, u : K_PASS // 2 : 2], ident[:])
+
+        def group_x(b, g, copy):
+            x_grouped[(b, g)] = stage.tile([P, 4 * S], BF16, name="x_grouped", align_bytes=64)
+            copy(
+                out=x_grouped[(b, g)][:].bitcast(F32).rearrange("p (j r u) -> p j r u", j=2, u=2),
+                in_=x_turned[(b, g)][:].rearrange("p j u r -> p j r u"),
             )
 
-        ident = keep.tile([P, P], F32, name="ident")
-        make_identity(nc, ident[:])
-        ident_bf = keep.tile([P, P], BF16, name="ident_bf")
-        nc.vector.tensor_copy(out=ident_bf[:], in_=ident[:])
-        split = keep.tile([P, 2, D // 2], F32, name="split")
-        nc.vector.tensor_copy(out=split[:], in_=ident[:].rearrange("p (f c) -> p c f", c=2))
+        def quantise_x(b, g):
+            cols = slice(S * b, S * (b + 1))
+            nc.vector.quantize_mx(
+                out=codes[g][:, cols].bitcast(E5M2X4), scales=x_scales[g][:, cols], in_=x_grouped[(b, g)][:]
+            )
 
-        codes, xscales = [], []
-        for g in range(PASSES):
-            code = keep.tile([P, TOKENS], U32, name="code%d" % g, align_bytes=64)
-            xscale = keep.tile([P, TOKENS], U8, name="xscale%d" % g, align_bytes=64)
-            codes.append(code)
-            xscales.append(xscale)
-        def prepare_x(g):
-            for b in range(B):
-                bank = psum.tile([P, 2, 2, P], F32, name="xbank", tag="t", bufs=4)
-                xw = x_sb[(g, b)][:].bitcast(F32)
-                for j in range(2):
-                    for u in range(2):
-                        nc.tensor.transpose(bank[:, j, u, :], xw[:, j, u:256:2], ident[:])
-                grouped = work.tile([P, 2 * P * 4], BF16, name="grouped", align_bytes=64)
-                nc.scalar.copy(
-                    out=grouped[:].bitcast(F32).rearrange("p (j r u) -> p j r u", j=2, u=2),
-                    in_=bank[:].rearrange("p j u r -> p j r u"),
-                )
-                cols = slice(256 * b, 256 * (b + 1))
-                nc.vector.quantize_mx(out=codes[g][:, cols].bitcast(E5M2X4), scales=xscales[g][:, cols], in_=grouped[:])
-
-        bias_col = keep.tile([P, NORMED_HEADS], F32, name="bias_col")
-
-        def prepare_bias():
-            if True:
-                bias_t = psum.tile([P, D], BF16, name="bias_t", tag="v")
-                nc.tensor.transpose(bias_t[:], rows[:], ident_bf[:])
-                nc.vector.tensor_copy(out=bias_col[:], in_=bias_t[:, 0:NORMED_HEADS])
-
+        bias_col = keep.tile([P, V0], F32, name="bias_col")
+        spread = keep.tile([P, H + 2, D], BF16, name="spread")
         table = keep.tile([P, 2, 2, 2 * D], F32, name="table")
 
-        def prepare_table(kind):
-            gain = gains[kind][:].rearrange("s (f c) -> s c f", c=2).unsqueeze(3).broadcast_to([P, 2, D // 2, 2])
+        def bias_columns(rows, h0, h1):
+            columns = bank([P, P], BF16, "turn")
+            nc.tensor.transpose(columns[:], rows[:], ident_bf[:])
+            nc.vector.tensor_copy(out=bias_col[:, h0:h1], in_=columns[:, 0 : h1 - h0])
+
+        def spread_rows(rows, first, m0, m1):
+            copies = bank([P, m1 - m0, D], BF16, "v")
+            for m in range(m1 - m0):
+                pick = ident_bf[:, first + m : first + m + 1].to_broadcast([P, P])
+                nc.tensor.matmul(copies[:, m, :], lhsT=pick, rhs=rows[:], start=True, stop=True)
+            nc.scalar.copy(out=spread[:, m0:m1, :], in_=copies[:])
+
+        def make_table(kind):
+            gain = spread[:, H + kind, :].rearrange("p (f c) -> p c f", c=2).unsqueeze(3).broadcast_to([P, 2, D // 2, 2])
             for j in range(2):
                 nc.vector.tensor_tensor(
-                    out=table[:, kind, j, :].rearrange("s (c f i) -> s c f i", c=2, i=2),
-                    in0=emb[:, j, :].rearrange("s (f i c) -> s c f i", i=2, c=2),
+                    out=table[:, kind, j, :].rearrange("p (c f i) -> p c f i", c=2, i=2),
+                    in0=emb[:, j, :].rearrange("p (f i c) -> p c f i", i=2, c=2),
                     in1=gain,
                     op=ALU.mult,
                 )
 
-        acc, y_t, turned, sumsq, rstd, prod, vacc, res = {}, {}, {}, {}, {}, {}, {}, {}
+        acc, biased, turned, sumsq, rstd, result, v_acc = {}, {}, {}, {}, {}, {}, {}
 
-        def project(h, passes=range(PASSES)):
-            if h not in acc:
-                acc[h] = psum.tile([P, TOKENS], F32, name="acc", tag="v" if 2 <= h < PRO else "f")
-            for g in passes:
-                w, ws = weight(D * h, D, g)
+        def groups(unit):
+            (h0, b0), (h1, b1) = unit
+            if h0 == h1:
+                return [(h0, slice(0, TOKENS), slice(0, TOKENS))]
+            return [(h, slice(S * m, S * (m + 1)), slice(S * b, S * (b + 1))) for m, (h, b) in enumerate(unit)]
+
+        def project(unit, first=0, last=2 * PASSES):
+            if first == 0:
+                acc[unit] = bank([P, TOKENS], F32, "unit")
+            calls = [(group, g) for group in groups(unit) for g in range(PASSES)]
+            for (h, cols, tokens), g in calls[first:last]:
+                w, w_scale = weight(h, 1, g)
                 nc.tensor.matmul_mx(
-                    out=acc[h][:], lhsT=w, lhsT_scale=ws, rhs=codes[g][:].bitcast(E5M2X4), rhs_scale=xscales[g][:],
-                    start=(g == 0), stop=(g == PASSES - 1),
+                    out=acc[unit][:, cols],
+                    lhsT=w,
+                    lhsT_scale=w_scale,
+                    rhs=codes[g][:, tokens].bitcast(E5M2X4),
+                    rhs_scale=x_scales[g][:, tokens],
+                    start=(g == 0),
+                    stop=(g == PASSES - 1),
                 )
 
-        def add_bias(h):
-            y_t[h] = work.tile([P, TOKENS], F32, name="y_t")
-            nc.scalar.activation(out=y_t[h][:], in_=acc[h][:], func=ACT.Identity, bias=bias_col[:, h : h + 1], scale=1.0)
-
-        def tiles_of(unit):
-            h, batches = unit
-            return [2 * b + j for b in batches for j in range(2)]
+        def add_bias(unit):
+            biased[unit] = stage.tile([P, TOKENS], F32, name="biased")
+            for h, cols, tokens in groups(unit):
+                nc.scalar.activation(
+                    out=biased[unit][:, cols], in_=acc[unit][:, cols], func=ACT.Identity, bias=bias_col[:, h : h + 1], scale=1.0
+                )
 
         def turn(unit):
-            tiles = tiles_of(unit)
-            turned[unit] = psum.tile([P, len(tiles), D], F32, name="turned", tag="t", bufs=4)
-            for n, t in enumerate(tiles):
+            turned[unit] = bank([P, TILES, D], F32, "turn")
+            for t in range(TILES):
                 nc.tensor.transpose(
-                    turned[unit][:, n, :], y_t[unit[0]][:, P * t : P * (t + 1)], split[:].rearrange("p c f -> p (c f)")
+                    turned[unit][:, t, :], biased[unit][:, P * t : P * (t + 1)], even_odd[:].rearrange("p c f -> p (c f)")
                 )
 
-        def squares(unit, lo, hi=4):
-            count = len(tiles_of(unit))
-            if unit not in sumsq:
-                sumsq[unit] = work.tile([P, count], F32, name="sumsq")
-            for n in range(lo, min(hi, count)):
-                squared = work.tile([P, D], F32, name="squared")
+        def squares(unit, first=0, last=TILES):
+            if first == 0:
+                sumsq[unit] = stage.tile([P, TILES], F32, name="sumsq")
+            for t in range(first, last):
+                squared = stage.tile([P, D], F32, name="squared")
                 nc.scalar.activation(
-                    out=squared[:], in_=turned[unit][:, n, :], func=ACT.Square, accum_out=sumsq[unit][:, n : n + 1]
+                    out=squared[:], in_=turned[unit][:, t, :], func=ACT.Square, accum_out=sumsq[unit][:, t : t + 1]
                 )
 
         def inverse_root(unit):
-            rstd[unit] = work.tile([P, len(tiles_of(unit))], F32, name="rstd")
-            nc.scalar.activation(
-                out=rstd[unit][:], in_=sumsq[unit][:], func=ACT.Abs_reciprocal_sqrt, scale=1.0 / D, bias=EPS
-            )
+            rstd[unit] = stage.tile([P, TILES], F32, name="rstd")
+            nc.scalar.activation(out=rstd[unit][:], in_=sumsq[unit][:], func=ACT.Abs_reciprocal_sqrt, scale=1.0 / D, bias=EPS)
 
-        def rope_products(unit):
-            tiles = tiles_of(unit)
-            prod[unit] = work.tile([P, len(tiles), 2, D], F32, name="prod")
-            for n, t in enumerate(tiles):
+        def rope(unit):
+            products = stage.tile([P, TILES, 2, D], F32, name="products")
+            for t in range(TILES):
                 nc.vector.scalar_tensor_tensor(
-                    out=prod[unit][:, n, :, :].rearrange("s c (f i) -> s (c f) i", i=2),
-                    in0=turned[unit][:, n, :].unsqueeze(2).broadcast_to([P, D, 2]),
-                    scalar=rstd[unit][:, n : n + 1],
-                    in1=table[:, unit[0] // H, t % 2, :].rearrange("s (m i) -> s m i", i=2),
+                    out=products[:, t, :, :].rearrange("p c (f i) -> p (c f) i", i=2),
+                    in0=turned[unit][:, t, :].unsqueeze(2).broadcast_to([P, D, 2]),
+                    scalar=rstd[unit][:, t : t + 1],
+                    in1=table[:, unit[0][0] // H, t % 2, :].rearrange("p (m i) -> p m i", i=2),
                     op0=ALU.mult,
                     op1=ALU.mult,
                 )
+            result[unit] = keep.tile([P, TILES, D], F32, name="result%d" % len(result))
+            nc.gpsimd.tensor_tensor(out=result[unit][:], in0=products[:, :, 0, :], in1=products[:, :, 1, :], op=ALU.add)
 
-        def rope_sum(unit, engine):
-            h, batches = unit
-            res[unit] = keep.tile([P, 2 * len(batches), D], F32, name="res%d_%d" % (h, batches[0]))
-            engine.tensor_tensor(out=res[unit][:], in0=prod[unit][:, :, 0, :], in1=prod[unit][:, :, 1, :], op=ALU.add)
-
-        def store_head(unit):
-            h, batches = unit
-            dst = (out_0, out_1)[h // H]
+        def store(unit):
+            (h0, b0), (h1, b1) = unit
+            out = (out_0, out_1)[h0 // H]
+            rows = out[:, h0 % H] if h0 == h1 else out[b0, h0 % H : h1 % H + 1]
             nc.sync.dma_start(
-                out=dst[batches[0] : batches[-1] + 1, h % H].rearrange("b (p j) d -> p b (j d)", j=2),
-                in_=res[unit][:].rearrange("p (b j) d -> p b (j d)", j=2),
+                out=rows.rearrange("m (p j) d -> p m (j d)", j=2),
+                in_=result[unit][:].rearrange("p (m j) d -> p m (j d)", j=2),
             )
 
-        def project_v(n, tag):
-            pair, b = divmod(n, B)
-            vacc[n] = psum.tile([P, 2, 2 * D], F32, name="vacc", tag=tag)
-            for j in range(2):
-                cols = slice(P * (2 * b + j), P * (2 * b + j + 1))
-                for g in range(PASSES):
-                    w, ws = weight(V0 + 2 * D * pair, 2 * D, g)
-                    nc.tensor.matmul_mx(
-                        out=vacc[n][:, j, :], lhsT=codes[g][:, cols].bitcast(E5M2X4), lhsT_scale=xscales[g][:, cols],
-                        rhs=w, rhs_scale=ws, start=(g == 0), stop=(g == PASSES - 1),
-                    )
+        def scalar_work(old, new):
+            squares(old[0])
+            for unit in old[1:]:
+                squares(unit, 0, 1)
+            inverse_root(old[0])
+            for unit in old[1:]:
+                squares(unit, 1)
+            for unit in new[:1]:
+                add_bias(unit)
+            for unit in old[1:]:
+                inverse_root(unit)
+            for unit in new[1:]:
+                add_bias(unit)
 
-        def finish_v(n):
-            pair, b = divmod(n, B)
-            vout = keep.tile([P, 2, 2, D], F32, name="vout%d" % n)
-            bias = bias_v[:, 2 * D * pair : 2 * D * (pair + 1)].rearrange("p (h d) -> p h d", d=D)
+        def project_v(item, j, role):
+            pair, b = item
+            if j == 0:
+                v_acc[item] = bank([P, 2, 2 * D], F32, role)
+            tokens = slice(S * b + P * j, S * b + P * (j + 1))
+            for g in range(PASSES):
+                w, w_scale = weight(V0 + 2 * pair, 2, g)
+                nc.tensor.matmul_mx(
+                    out=v_acc[item][:, j, :],
+                    lhsT=codes[g][:, tokens].bitcast(E5M2X4),
+                    lhsT_scale=x_scales[g][:, tokens],
+                    rhs=w,
+                    rhs_scale=w_scale,
+                    start=(g == 0),
+                    stop=(g == PASSES - 1),
+                )
+
+        def finish_v(item):
+            pair, b = item
+            v_out = keep.tile([P, 2, 2, D], F32, name="v_out%d%d" % item)
             nc.vector.tensor_tensor(
-                out=vout[:],
-                in0=vacc[n][:].rearrange("p j (h d) -> p h j d", d=D),
-                in1=bias.unsqueeze(2).broadcast_to([P, 2, 2, D]),
+                out=v_out[:],
+                in0=v_acc[item][:].rearrange("p j (h d) -> p h j d", d=D),
+                in1=spread[:, 2 * pair : 2 * (pair + 1), :].unsqueeze(2).broadcast_to([P, 2, 2, D]),
                 op=ALU.add,
             )
             nc.sync.dma_start(
                 out=out_2[b, 2 * pair : 2 * (pair + 1)].rearrange("h (p j) d -> p h (j d)", j=2),
-                in_=vout[:].rearrange("p h j d -> p h (j d)"),
+                in_=v_out[:].rearrange("p h j d -> p h (j d)"),
             )
 
-        prepare_x(0)
-        prepare_x(1)
-        prepare_bias()
-        early = 2 if X_FIRST < PASSES else 0
-        for h in range(early):
-            project(h, [0])
-        prepare_x(2)
-        prepare_table(0)
-        prepare_table(1)
-        for h in range(early, PRO):
-            project(h, [0])
-        for g in range(1, PASSES):
-            for h in range(PRO):
-                project(h, [g])
-        for h in range(AHEAD):
-            add_bias(h)
-        first = 0
-        old = []
-        next_v = 0
-        for r, n_v in enumerate(V_PER_RUN):
-            last = r == len(RUNS)
-            run = [] if last else list(range(first, first + RUNS[r]))
-            first += len(run)
-            new = [h + AHEAD for h in run if h + AHEAD < NORMED_HEADS]
-            run = [(h, (0, 1)) for h in run]
-            if r == len(RUNS) - 1:
-                run = run[:-1] + [(NORMED_HEADS - 1, (b,)) for b in range(B)]
-            vs = list(range(next_v, next_v + n_v))
-            next_v += n_v
-            todo_v = list(vs)
-            pending_store = []
-            done_v = 0
-            for m in range(max(len(old), len(new), 1)):
-                if m == 0:
-                    for h in new[:2]:
-                        if h not in acc:
-                            project(h)
-                    if len(new) < 2 and todo_v and not EARLY_TURN:
-                        n = todo_v.pop(0)
-                        project_v(n, "v")
-                elif m + 1 < len(new):
-                    if todo_v:
-                        n = todo_v.pop(0)
-                        project_v(n, "v")
-                    if new[m + 1] not in acc:
-                        project(new[m + 1])
-                if m == 0 and old:
-                    squares(old[0], 0)
-                    if len(old) > 1:
-                        squares(old[1], 0, 1)
-                    inverse_root(old[0])
-                    if len(old) > 1:
-                        squares(old[1], 1)
-                elif 0 < m and m + 1 < len(old):
-                    squares(old[m + 1], 0)
-                if m < len(new):
-                    add_bias(new[m])
-                if m + 1 < len(old):
-                    inverse_root(old[m + 1])
-                if m < len(old):
-                    if last and m == 0 and TAIL_V_FIRST:
-                        for n in vs:
-                            project_v(n, "f")
-                            finish_v(n)
-                        vs, todo_v = [], []
-                    rope_products(old[m])
-                    rope_sum(old[m], nc.vector if last and m == len(old) - 1 else nc.gpsimd)
-                    if m + 1 < len(old) or not vs or last:
-                        store_head(old[m])
-                    else:
-                        pending_store.append(old[m])
-            for k, n in enumerate(todo_v):
-                project_v(n, "f" if (last and k % 2 == 0) else "v")
-            for h in run:
-                turn(h)
-            for n in vs[:1]:
-                finish_v(n)
-            for h in pending_store:
-                store_head(h)
-            for n in vs[1:]:
-                finish_v(n)
+        units = [((h, b), (h + 1, b)) for b in range(B) for h in range(K0, K0 + EARLY, 2)]
+        units += [((h, 0), (h, 1)) for h in list(range(K0 + EARLY, V0)) + list(range(K0))]
+        v_banks = [(pair, b) for pair in range(H // 2) for b in range(B)]
+
+        for m0 in (0, H // 2):
+            spread_rows(first_rows, V0 - LATE_ROWS + m0, m0, m0 + H // 2)
+        turn_x(0, 0)
+        group_x(0, 0, nc.scalar.copy)
+        quantise_x(0, 0)
+        turn_x(0, 1)
+        turn_x(0, 2)
+        group_x(0, 1, nc.scalar.copy)
+        group_x(0, 2, nc.vector.tensor_copy)
+        quantise_x(0, 1)
+        quantise_x(0, 2)
+        bias_columns(first_rows, LATE_ROWS, V0)
+        bias_columns(late_rows, 0, LATE_ROWS)
+        spread_rows(late_rows, LATE_ROWS, H, H + 2)
+        for g in range(PASSES - 1):
+            project(units[0], g, g + 1)
+            project(units[1], g, g + 1)
+        project(units[0], PASSES - 1)
+        make_table(1)
+        make_table(0)
+        add_bias(units[0])
+
+        turn_x(1, 0)
+        turn_x(1, 1)
+        turn(units[0])
+        group_x(1, 0, nc.vector.tensor_copy)
+        group_x(1, 1, nc.vector.tensor_copy)
+        turn_x(1, 2)
+        quantise_x(1, 0)
+        group_x(1, 2, nc.vector.tensor_copy)
+        quantise_x(1, 1)
+        scalar_work([units[0]], [])
+        project(units[1], PASSES - 1)
+        quantise_x(1, 2)
+        add_bias(units[1])
+        for j in range(2):
+            project_v(v_banks[0], j, "v")
+        project(units[2])
+        add_bias(units[2])
+        turn(units[1])
+        rope(units[0])
+        finish_v(v_banks[0])
+        store(units[0])
+
+        halves = [(item, j) for item in v_banks[1:] for j in range(2)]
+        old = [units[1]]
+        for n in range(2, len(units), 2):
+            run, new = units[n : n + 2], units[n + 1 : n + 3]
+            count = 1 + len(run) - len(new)
+            now, halves = halves[:count], halves[count:]
+            full = [item for item, j in now if j == 1]
+            for unit in new:
+                project(unit)
+            for item, j in now:
+                project_v(item, j, "v")
+            scalar_work(old, new)
+            for unit in run:
+                turn(unit)
+            for unit in old[:-1]:
+                rope(unit)
+                store(unit)
+            rope(old[-1])
+            for item in full:
+                finish_v(item)
+            store(old[-1])
             old = run
+
+        rest = [item for item, j in halves if j == 0]
+        for item, role in zip(rest, ("unit", "unit", "turn", "turn", "v")):
+            for j in range(2):
+                project_v(item, j, role)
+        scalar_work(old, [])
+        finish_v(rest[0])
+        rope(old[0])
+        finish_v(rest[1])
+        rope(old[1])
+        store(old[0])
+        finish_v(rest[2])
+        finish_v(rest[3])
+        store(old[1])
+        finish_v(rest[4])

from contextlib import ExitStack

import concourse.mybir as mybir
from concourse.masks import make_identity

B, S, H, D = 2, 256, 12, 128
DIM = H * D
EPS = 1e-6
FLOPS = 2 * B * S * DIM * 3 * DIM

F32 = mybir.dt.float32
BF16 = mybir.dt.bfloat16
I32 = mybir.dt.int32
U32 = mybir.dt.uint32
U8 = mybir.dt.uint8
E5M2X4 = mybir.dt.float8_e5m2_x4
E2M1X4 = mybir.dt.float4_e2m1fn_x4
ACT = mybir.ActivationFunctionType
ALU = mybir.AluOpType

P = 128
K_PASS = 512
PASSES = DIM // K_PASS
TOKENS = B * S
TILES = TOKENS // P
K0, V0, HEADS = H, 2 * H, 3 * H

EARLY = 4
CHUNKS = [(K0, K0 + EARLY), (V0, V0 + EARLY), (K0 + EARLY, V0), (0, K0), (V0 + EARLY, HEADS)]
QUADRANT = 32
LATE_ROWS = HEADS - QUADRANT
BANKS = {"turn": 4, "unit": 2, "v": 2}
STAGE_BUFS = 4


def tile_fluxsingleattention_pa_kernel(
    tc, hidden_states, image_rotary_emb, w_qkv_words, w_qkv_scales, b_qkv, norm_q_w, norm_k_w, out_0, out_1, out_2
):
    nc = tc.nc
    with ExitStack() as ctx:
        keep = ctx.enter_context(tc.tile_pool(name="keep", bufs=1))
        stage = ctx.enter_context(tc.tile_pool(name="stage", bufs=STAGE_BUFS))
        psum = ctx.enter_context(tc.psum_pool(name="psum", bufs=1))
        ctx.enter_context(tc.manual_schedule())

        def bank(shape, dtype, role):
            return psum.tile(shape, dtype, name="bank_" + role, tag=role, bufs=BANKS[role])

        bias_by_head = b_qkv.rearrange("(h d) -> h d", d=D)
        first_rows = keep.tile([P, D], BF16, name="first_rows")
        late_rows = keep.tile([P, D], BF16, name="late_rows")
        nc.sync.dma_start(out=first_rows[0:QUADRANT, :], in_=bias_by_head[LATE_ROWS:HEADS, :])
        nc.vector.memset(first_rows[QUADRANT : 2 * QUADRANT, :].bitcast(I32), 0)
        nc.vector.memset(first_rows[2 * QUADRANT : P, :].bitcast(I32), 0)
        nc.vector.memset(late_rows[:].bitcast(I32), 0)

        planes, words = [], []
        for n, (h0, h1) in enumerate(CHUNKS):
            planes.append(keep.tile([P, PASSES, D * (h1 - h0)], U8, name="plane%d" % n, align_bytes=64))
            words.append(keep.tile([P, PASSES, 2 * D * (h1 - h0)], U8, name="words%d" % n, align_bytes=64))

        def clear_plane(n):
            nc.vector.memset(planes[n][:].rearrange("p g n -> p (g n)").bitcast(I32), 0)

        clear_plane(0)
        ident = keep.tile([P, P], F32, name="ident")
        make_identity(nc, ident[:])
        clear_plane(1)
        ident_bf = keep.tile([P, P], BF16, name="ident_bf")
        nc.vector.tensor_copy(out=ident_bf[:], in_=ident[:])
        for n in range(2, len(CHUNKS)):
            clear_plane(n)

        x_pairs = {}

        def load_x(b, g0, g1):
            x_sb = keep.tile([P, 2, K_PASS * (g1 - g0)], BF16, name="x%d%d" % (b, g0), align_bytes=64)
            tokens = hidden_states[b].rearrange("(p j) k -> p j k", j=2)
            nc.sync.dma_start(out=x_sb[:], in_=tokens[:, :, K_PASS * g0 : K_PASS * g1])
            width = K_PASS // 2
            for g in range(g0, g1):
                x_pairs[(b, g)] = x_sb[:].bitcast(F32)[:, :, width * (g - g0) : width * (g - g0 + 1)]

        def load_scales(n):
            h0, h1 = CHUNKS[n]
            for r in range(4):
                nc.sync.dma_start(
                    out=planes[n][r:P:QUADRANT, :, :].bitcast(I32),
                    in_=w_qkv_scales[:, r:16:4, D * h0 : D * h1].rearrange("g q n -> q g n").bitcast(I32),
                )

        def load_words(n):
            h0, h1 = CHUNKS[n]
            nc.sync.dma_start(
                out=words[n][:].bitcast(I32),
                in_=w_qkv_words[:, :, 2 * D * h0 : 2 * D * h1].rearrange("g p n -> p g n").bitcast(I32),
            )

        load_x(0, 0, 1)
        load_x(0, 1, PASSES)
        load_scales(0)
        load_words(0)
        nc.sync.dma_start(out=late_rows[0:LATE_ROWS, :], in_=bias_by_head[0:LATE_ROWS, :])
        for kind, gain in enumerate((norm_q_w, norm_k_w)):
            row = LATE_ROWS + kind
            nc.sync.dma_start(out=late_rows[row : row + 1, :], in_=gain.rearrange("(r d) -> r d", r=1))
        emb = keep.tile([P, 2, 2 * D], BF16, name="emb")
        nc.sync.dma_start(out=emb[:], in_=image_rotary_emb[0, 0].rearrange("(p j) f i c -> p j (f i c)", j=2))
        load_x(1, 0, PASSES)
        for n in (1, 2):
            load_scales(n)
            load_words(n)
        for n in (3, 4):
            load_scales(n)
        for n in (3, 4):
            load_words(n)

        even_odd = keep.tile([P, 2, D // 2], F32, name="even_odd")
        nc.scalar.activation(out=even_odd[:], in_=ident[:].rearrange("p (f c) -> p c f", c=2), func=ACT.Copy)

        def weight(head, count, g):
            n = [m for m, (h0, h1) in enumerate(CHUNKS) if h0 <= head < h1][0]
            c0 = D * (head - CHUNKS[n][0])
            c1 = c0 + D * count
            return words[n][:, g, 2 * c0 : 2 * c1].bitcast(E2M1X4), planes[n][:, g, c0:c1]

        codes, x_scales = [], []
        for g in range(PASSES):
            codes.append(keep.tile([P, TOKENS], U32, name="codes%d" % g, align_bytes=64))
            x_scales.append(keep.tile([P, TOKENS], U8, name="x_scales%d" % g, align_bytes=64))
        x_turned, x_grouped = {}, {}

        def turn_x(b, g):
            x_turned[(b, g)] = bank([P, 2, 2, P], F32, "turn")
            for j in range(2):
                for u in range(2):
                    nc.tensor.transpose(x_turned[(b, g)][:, j, u, :], x_pairs[(b, g)][:, j, u : K_PASS // 2 : 2], ident[:])

        def group_x(b, g, copy):
            x_grouped[(b, g)] = stage.tile([P, 4 * S], BF16, name="x_grouped", align_bytes=64)
            copy(
                out=x_grouped[(b, g)][:].bitcast(F32).rearrange("p (j r u) -> p j r u", j=2, u=2),
                in_=x_turned[(b, g)][:].rearrange("p j u r -> p j r u"),
            )

        def quantise_x(b, g):
            cols = slice(S * b, S * (b + 1))
            nc.vector.quantize_mx(
                out=codes[g][:, cols].bitcast(E5M2X4), scales=x_scales[g][:, cols], in_=x_grouped[(b, g)][:]
            )

        bias_col = keep.tile([P, V0], F32, name="bias_col")
        spread = keep.tile([P, H + 2, D], BF16, name="spread")
        table = keep.tile([P, 2, 2, 2 * D], F32, name="table")

        def bias_columns(rows, h0, h1):
            columns = bank([P, P], BF16, "turn")
            nc.tensor.transpose(columns[:], rows[:], ident_bf[:])
            nc.vector.tensor_copy(out=bias_col[:, h0:h1], in_=columns[:, 0 : h1 - h0])

        def spread_rows(rows, first, m0, m1):
            copies = bank([P, m1 - m0, D], BF16, "v")
            for m in range(m1 - m0):
                pick = ident_bf[:, first + m : first + m + 1].to_broadcast([P, P])
                nc.tensor.matmul(copies[:, m, :], lhsT=pick, rhs=rows[:], start=True, stop=True)
            nc.scalar.copy(out=spread[:, m0:m1, :], in_=copies[:])

        def make_table(kind):
            gain = spread[:, H + kind, :].rearrange("p (f c) -> p c f", c=2).unsqueeze(3).broadcast_to([P, 2, D // 2, 2])
            for j in range(2):
                nc.vector.tensor_tensor(
                    out=table[:, kind, j, :].rearrange("p (c f i) -> p c f i", c=2, i=2),
                    in0=emb[:, j, :].rearrange("p (f i c) -> p c f i", i=2, c=2),
                    in1=gain,
                    op=ALU.mult,
                )

        acc, biased, turned, sumsq, rstd, result, v_acc = {}, {}, {}, {}, {}, {}, {}

        def groups(unit):
            (h0, b0), (h1, b1) = unit
            if h0 == h1:
                return [(h0, slice(0, TOKENS), slice(0, TOKENS))]
            return [(h, slice(S * m, S * (m + 1)), slice(S * b, S * (b + 1))) for m, (h, b) in enumerate(unit)]

        def project(unit, first=0, last=2 * PASSES):
            if first == 0:
                acc[unit] = bank([P, TOKENS], F32, "unit")
            calls = [(group, g) for group in groups(unit) for g in range(PASSES)]
            for (h, cols, tokens), g in calls[first:last]:
                w, w_scale = weight(h, 1, g)
                nc.tensor.matmul_mx(
                    out=acc[unit][:, cols],
                    lhsT=w,
                    lhsT_scale=w_scale,
                    rhs=codes[g][:, tokens].bitcast(E5M2X4),
                    rhs_scale=x_scales[g][:, tokens],
                    start=(g == 0),
                    stop=(g == PASSES - 1),
                )

        def add_bias(unit):
            biased[unit] = stage.tile([P, TOKENS], F32, name="biased")
            for h, cols, tokens in groups(unit):
                nc.scalar.activation(
                    out=biased[unit][:, cols], in_=acc[unit][:, cols], func=ACT.Identity, bias=bias_col[:, h : h + 1], scale=1.0
                )

        def turn(unit):
            turned[unit] = bank([P, TILES, D], F32, "turn")
            for t in range(TILES):
                nc.tensor.transpose(
                    turned[unit][:, t, :], biased[unit][:, P * t : P * (t + 1)], even_odd[:].rearrange("p c f -> p (c f)")
                )

        def squares(unit, first=0, last=TILES):
            if first == 0:
                sumsq[unit] = stage.tile([P, TILES], F32, name="sumsq")
            for t in range(first, last):
                squared = stage.tile([P, D], F32, name="squared")
                nc.scalar.activation(
                    out=squared[:], in_=turned[unit][:, t, :], func=ACT.Square, accum_out=sumsq[unit][:, t : t + 1]
                )

        def inverse_root(unit):
            rstd[unit] = stage.tile([P, TILES], F32, name="rstd")
            nc.scalar.activation(out=rstd[unit][:], in_=sumsq[unit][:], func=ACT.Abs_reciprocal_sqrt, scale=1.0 / D, bias=EPS)

        def rope(unit):
            products = stage.tile([P, TILES, 2, D], F32, name="products")
            for t in range(TILES):
                nc.vector.scalar_tensor_tensor(
                    out=products[:, t, :, :].rearrange("p c (f i) -> p (c f) i", i=2),
                    in0=turned[unit][:, t, :].unsqueeze(2).broadcast_to([P, D, 2]),
                    scalar=rstd[unit][:, t : t + 1],
                    in1=table[:, unit[0][0] // H, t % 2, :].rearrange("p (m i) -> p m i", i=2),
                    op0=ALU.mult,
                    op1=ALU.mult,
                )
            result[unit] = keep.tile([P, TILES, D], F32, name="result%d" % len(result))
            nc.gpsimd.tensor_tensor(out=result[unit][:], in0=products[:, :, 0, :], in1=products[:, :, 1, :], op=ALU.add)

        def store(unit):
            (h0, b0), (h1, b1) = unit
            out = (out_0, out_1)[h0 // H]
            rows = out[:, h0 % H] if h0 == h1 else out[b0, h0 % H : h1 % H + 1]
            nc.sync.dma_start(
                out=rows.rearrange("m (p j) d -> p m (j d)", j=2),
                in_=result[unit][:].rearrange("p (m j) d -> p m (j d)", j=2),
            )

        def scalar_work(old, new):
            squares(old[0])
            for unit in old[1:]:
                squares(unit, 0, 1)
            inverse_root(old[0])
            for unit in old[1:]:
                squares(unit, 1)
            for unit in new[:1]:
                add_bias(unit)
            for unit in old[1:]:
                inverse_root(unit)
            for unit in new[1:]:
                add_bias(unit)

        def project_v(item, j, role):
            pair, b = item
            if j == 0:
                v_acc[item] = bank([P, 2, 2 * D], F32, role)
            tokens = slice(S * b + P * j, S * b + P * (j + 1))
            for g in range(PASSES):
                w, w_scale = weight(V0 + 2 * pair, 2, g)
                nc.tensor.matmul_mx(
                    out=v_acc[item][:, j, :],
                    lhsT=codes[g][:, tokens].bitcast(E5M2X4),
                    lhsT_scale=x_scales[g][:, tokens],
                    rhs=w,
                    rhs_scale=w_scale,
                    start=(g == 0),
                    stop=(g == PASSES - 1),
                )

        def finish_v(item):
            pair, b = item
            v_out = keep.tile([P, 2, 2, D], F32, name="v_out%d%d" % item)
            nc.vector.tensor_tensor(
                out=v_out[:],
                in0=v_acc[item][:].rearrange("p j (h d) -> p h j d", d=D),
                in1=spread[:, 2 * pair : 2 * (pair + 1), :].unsqueeze(2).broadcast_to([P, 2, 2, D]),
                op=ALU.add,
            )
            nc.sync.dma_start(
                out=out_2[b, 2 * pair : 2 * (pair + 1)].rearrange("h (p j) d -> p h (j d)", j=2),
                in_=v_out[:].rearrange("p h j d -> p h (j d)"),
            )

        units = [((h, b), (h + 1, b)) for b in range(B) for h in range(K0, K0 + EARLY, 2)]
        units += [((h, 0), (h, 1)) for h in list(range(K0 + EARLY, V0)) + list(range(K0))]
        v_banks = [(pair, b) for pair in range(H // 2) for b in range(B)]

        for m0 in (0, H // 2):
            spread_rows(first_rows, V0 - LATE_ROWS + m0, m0, m0 + H // 2)
        turn_x(0, 0)
        group_x(0, 0, nc.scalar.copy)
        quantise_x(0, 0)
        turn_x(0, 1)
        turn_x(0, 2)
        group_x(0, 1, nc.scalar.copy)
        group_x(0, 2, nc.vector.tensor_copy)
        quantise_x(0, 1)
        quantise_x(0, 2)
        bias_columns(first_rows, LATE_ROWS, V0)
        bias_columns(late_rows, 0, LATE_ROWS)
        spread_rows(late_rows, LATE_ROWS, H, H + 2)
        for g in range(PASSES - 1):
            project(units[0], g, g + 1)
            project(units[1], g, g + 1)
        project(units[0], PASSES - 1)
        make_table(1)
        make_table(0)
        add_bias(units[0])

        turn_x(1, 0)
        turn_x(1, 1)
        turn(units[0])
        group_x(1, 0, nc.vector.tensor_copy)
        group_x(1, 1, nc.vector.tensor_copy)
        turn_x(1, 2)
        quantise_x(1, 0)
        group_x(1, 2, nc.vector.tensor_copy)
        quantise_x(1, 1)
        scalar_work([units[0]], [])
        project(units[1], PASSES - 1)
        quantise_x(1, 2)
        add_bias(units[1])
        for j in range(2):
            project_v(v_banks[0], j, "v")
        project(units[2])
        add_bias(units[2])
        turn(units[1])
        rope(units[0])
        finish_v(v_banks[0])
        store(units[0])

        halves = [(item, j) for item in v_banks[1:] for j in range(2)]
        old = [units[1]]
        for n in range(2, len(units), 2):
            run, new = units[n : n + 2], units[n + 1 : n + 3]
            count = 1 + len(run) - len(new)
            now, halves = halves[:count], halves[count:]
            full = [item for item, j in now if j == 1]
            for unit in new:
                project(unit)
            for item, j in now:
                project_v(item, j, "v")
            scalar_work(old, new)
            for unit in run:
                turn(unit)
            for unit in old[:-1]:
                rope(unit)
                store(unit)
            rope(old[-1])
            for item in full:
                finish_v(item)
            store(old[-1])
            old = run

        rest = [item for item, j in halves if j == 0]
        for item, role in zip(rest, ("unit", "unit", "turn", "turn", "v")):
            for j in range(2):
                project_v(item, j, role)
        scalar_work(old, [])
        finish_v(rest[0])
        rope(old[0])
        finish_v(rest[1])
        rope(old[1])
        store(old[0])
        finish_v(rest[2])
        finish_v(rest[3])
        store(old[1])
        finish_v(rest[4])
